import numpy as np
import ml_dtypes


def mxq(x, axis, fmt="e4m3"):
    dtype, down = {"e4m3": (ml_dtypes.float8_e4m3fn, 7), "e5m2": (ml_dtypes.float8_e5m2, 14)}[fmt]
    v = np.moveaxis(np.asarray(x, np.float32).astype(ml_dtypes.bfloat16).astype(np.float64), axis, -1)
    blocks = v.reshape(v.shape[:-1] + (-1, 32))
    amax = np.abs(blocks).max(-1, keepdims=True)
    byte = np.maximum(np.where(amax > 0, np.frexp(amax)[1] - 1 + 127, 0) - down, 1)
    scale = np.exp2(byte - 127.0)
    codes = (blocks / scale).astype(np.float32).astype(dtype).astype(np.float64)
    return np.moveaxis((codes * scale).reshape(v.shape), -1, axis)


WIDE = False


def mx_kscale(k):
    if not WIDE:
        return np.ones(k)
    levels = np.array([10, -10, 5, -5, 0])
    a = np.random.permutation(np.resize(levels, k // 512 * 4)).reshape(k // 512, 4)
    idx = np.arange(k)
    return np.exp2(a[idx // 512, idx % 128 // 32])


BF16 = ml_dtypes.bfloat16


def bf(x):
    return np.asarray(x, np.float32).astype(BF16)


def f64(x):
    return np.asarray(x).astype(np.float64)


B, N, D, O, M = 4, 512, 768, 768, 4
KW = D * M


def draw_support():
    m = np.exp(2.0 * np.random.standard_normal((N, N)) - 2.0) * (3.0 / N) + np.eye(N)
    d = m.sum(axis=1) ** -0.5
    return (m * d[None, :]).T * d[None, :]


def setup_inputs():
    u = mx_kscale(KW)[::M]
    return {"x0": bf(np.random.standard_normal((B, N, D)) * u),
            "x1": bf(np.random.standard_normal((B, N, D)) * 0.4 * u),
            "x2": bf(np.random.standard_normal((B, N, D)) * 0.9 * u),
            "support": bf(draw_support()),
            "weights": bf(np.random.standard_normal((KW, O)) / np.sqrt(KW) / np.repeat(u, M)[:, None]),
            "biases": bf(np.random.standard_normal(O) * 0.3)}


def reference(x0, x1, x2, support, weights, biases):
    x0, x1, x2 = f64(x0), f64(x1), f64(x2)
    x3 = 2.0 * (mxq(f64(support), 1, "e4m3") @ mxq(x2, 1, "e4m3")) - x1
    x = np.stack([x0, x1, x2, x3], axis=-1).reshape(B * N, KW)
    out = (mxq(x, 1, "e4m3") @ mxq(f64(weights), 0, "e4m3")) + f64(biases)
    return out.reshape(B, N, O)

@@ -1,0 +1,280 @@
+from contextlib import ExitStack
+
+import concourse.mybir as mybir
+from concourse.masks import make_identity
+
+FP8X4 = mybir.dt.float8_e4m3fn_x4
+BF16 = mybir.dt.bfloat16
+F32 = mybir.dt.float32
+U32 = mybir.dt.uint32
+U8 = mybir.dt.uint8
+ALU = mybir.AluOpType
+
+P = 128
+B, N, D, O, M = 4, 512, 768, 768, 4
+NT = N // P
+G = D // P
+TILES = B * NT
+LAG = 2
+HALVES = ((0, 512), (512, 768))
+FLOPS = 2 * B * N * N * D + 2 * B * N * D * M * O
+
+
+def tile_dgcn_pb_kernel(tc, x0, x1, x2, support, weights, biases, out):
+    nc = tc.nc
+    with ExitStack() as ctx:
+        const = ctx.enter_context(tc.tile_pool(name="const", bufs=1))
+        big = ctx.enter_context(tc.tile_pool(name="big", bufs=12))
+        work = ctx.enter_context(tc.tile_pool(name="work", bufs=2))
+        psum = ctx.enter_context(tc.psum_pool(name="psum", bufs=2))
+        ctx.enter_context(tc.manual_schedule())
+
+        sup = const.tile([P, NT, N], BF16, name="sup")
+        nc.sync.dma_start(out=sup[:], in_=support.rearrange("(p t) j -> p t j", t=NT))
+        xs = {}
+        srcs = (x0, x1, x2)
+        wraw = {}
+
+        def load_x(m, b):
+            xt = big.tile([P, NT, D], BF16, name="x%d_%d" % (m, b), tag="big")
+            nc.sync.dma_start(out=xt[:], in_=srcs[m][b].rearrange("(p t) d -> p t d", t=NT))
+            xs[(m, b)] = xt
+
+        def load_w(g):
+            wr = big.tile([P, M, O], BF16, name="wraw%d" % g, tag="big")
+            nc.sync.dma_start(
+                out=wr[:],
+                in_=weights[g * P * M:(g + 1) * P * M, :].rearrange("(p t) o -> p t o", t=M),
+            )
+            wraw[g] = wr
+
+        load_x(2, 0)
+        load_w(0)
+        load_x(1, 0)
+        load_x(0, 0)
+        for g in range(1, G):
+            load_w(g)
+        for m in (2, 1, 0):
+            load_x(m, 1)
+        bias_bc = const.tile([P, O], BF16, name="bias_bc")
+        nc.sync.dma_start(out=bias_bc[:], in_=biases.partition_broadcast(P))
+        for b in range(2, B):
+            for m in (2, 1, 0):
+                load_x(m, b)
+
+        ident_f = const.tile([P, P], F32, name="ident_f")
+        make_identity(nc, ident_f[:])
+        ident_bf = const.tile([P, P], BF16, name="ident_bf")
+        make_identity(nc, ident_bf[:])
+
+        supg = const.tile([P, NT * P * 4], BF16, name="supg", align_bytes=64)
+        sup_codes = const.tile([P, N], U32, name="sup_codes", align_bytes=64)
+        sup_scales = const.tile([P, N], U8, name="sup_scales", align_bytes=64)
+        sup_words = sup[:].bitcast(F32).rearrange("p t (q u) -> p t u q", u=2)
+        supg_words = supg[:].bitcast(F32).rearrange("q (t p u) -> q t p u", t=NT, u=2)
+        for half in range(2):
+            st = psum.tile([P, 2, 2, P], F32, name="st", tag="g", bufs=4)
+            for tt in range(2):
+                for u in range(2):
+                    nc.tensor.transpose(st[:, tt, u, :], sup_words[:, 2 * half + tt, u, :], ident_f[:])
+            nc.scalar.copy(
+                out=supg_words[:, 2 * half:2 * half + 2, :, :],
+                in_=st[:].rearrange("q t u p -> q t p u"),
+            )
+        nc.vector.quantize_mx(out=sup_codes[:].bitcast(FP8X4), scales=sup_scales[:], in_=supg[:])
+
+        def regroup(engine, dst, src, lo, hi):
+            o_ap = dst[:, lo:hi, :].rearrange("p (c i) t -> p c t i", i=4)
+            i_ap = src[:, :, lo:hi].rearrange("p t (c i) -> p c t i", i=4)
+            if engine == "v":
+                nc.vector.tensor_copy(out=o_ap, in_=i_ap)
+            else:
+                nc.scalar.copy(out=o_ap, in_=i_ap)
+
+        def quantise(codes, scales, src):
+            for lo, hi in HALVES:
+                nc.vector.quantize_mx(
+                    out=codes[:, lo:hi].bitcast(FP8X4),
+                    scales=scales[:, lo:hi],
+                    in_=src[:, lo:hi, :].rearrange("p c t -> p (c t)"),
+                )
+
+        x2gs = {}
+        x2q = {}
+
+        def x2_regroup(b, engines):
+            x2g = work.tile([P, D, 4], BF16, name="x2g", align_bytes=64)
+            for engine, (lo, hi) in zip(engines, HALVES):
+                regroup(engine, x2g, xs[(2, b)], lo, hi)
+            x2gs[b] = x2g
+
+        def x2_quantise(b):
+            c = work.tile([P, D], U32, name="x2codes", align_bytes=64)
+            s = work.tile([P, D], U8, name="x2scales", align_bytes=64)
+            quantise(c, s, x2gs[b])
+            x2q[b] = (c, s)
+
+        wcodes = const.tile([P, G, O], U32, name="wcodes", align_bytes=64)
+        wscales = const.tile([P, G, O], U8, name="wscales", align_bytes=64)
+        wgs = {}
+
+        def w_regroup(g, engine):
+            wg = work.tile([P, O, 4], BF16, name="wg", bufs=4, align_bytes=64)
+            for lo, hi in HALVES:
+                regroup(engine, wg, wraw[g], lo, hi)
+            wgs[g] = wg
+
+        def w_quantise(g):
+            quantise(wcodes[:, g, :], wscales[:, g, :], wgs[g])
+
+        x3s = {}
+        accs = {}
+
+        def new_acc():
+            acc_a = psum.tile([P, 512], F32, name="acc_a")
+            acc_b = psum.tile([P, 256], F32, name="acc_b")
+            return acc_a, acc_b
+
+        def s1(i):
+            b, t = divmod(i, NT)
+            c, s = x2q[b]
+            acc = new_acc()
+            for k, (lo, hi) in enumerate(HALVES):
+                nc.tensor.matmul_mx(
+                    out=acc[k][:],
+                    lhsT=sup_codes[:, t * P:(t + 1) * P].bitcast(FP8X4),
+                    lhsT_scale=sup_scales[:, t * P:(t + 1) * P],
+                    rhs=c[:, lo:hi].bitcast(FP8X4),
+                    rhs_scale=s[:, lo:hi],
+                    start=True,
+                    stop=True,
+                )
+            accs[("s1", i)] = acc
+
+        def x3(i):
+            b, t = divmod(i, NT)
+            if t == 0:
+                x3s[b] = work.tile([P, NT, D], BF16, name="x3t")
+            acc = accs[("s1", i)]
+            for k, (lo, hi) in enumerate(HALVES):
+                nc.vector.scalar_tensor_tensor(
+                    out=x3s[b][:, t, lo:hi],
+                    in0=acc[k][:],
+                    scalar=2.0,
+                    in1=xs[(1, b)][:, t, lo:hi],
+                    op0=ALU.mult,
+                    op1=ALU.subtract,
+                )
+
+        grouped = {}
+
+        def transposes(i):
+            b, t = divmod(i, NT)
+            gr = work.tile([P, G, P, 4], BF16, name="grouped", bufs=4, align_bytes=64)
+            grouped[i] = gr
+            for gp in range(G // 2):
+                bank = psum.tile([P, 2, 4, P], BF16, name="bank", tag="g", bufs=4)
+                for u in range(2):
+                    g = 2 * gp + u
+                    for m in range(4):
+                        src = xs[(m, b)] if m < 3 else x3s[b]
+                        nc.tensor.transpose(bank[:, u, m, :], src[:, t, g * P:(g + 1) * P], ident_bf[:])
+                nc.scalar.copy(
+                    out=gr[:, 2 * gp:2 * gp + 2, :, :],
+                    in_=bank[:].rearrange("p u m r -> p u r m"),
+                )
+
+        xq = {}
+
+        def qx(i):
+            c = work.tile([P, G * P], U32, name="xcodes", bufs=4, align_bytes=64)
+            s = work.tile([P, G * P], U8, name="xscales", bufs=4, align_bytes=64)
+            quantise(c, s, grouped[i][:].rearrange("p g r m -> p (g r) m"))
+            xq[i] = (c, s)
+
+        def s2_pass(i, g, k):
+            c, s = xq[i]
+            lo, hi = HALVES[k]
+            nc.tensor.matmul_mx(
+                out=accs[("s2", i)][k][:],
+                lhsT=c[:, g * P:(g + 1) * P].bitcast(FP8X4),
+                lhsT_scale=s[:, g * P:(g + 1) * P],
+                rhs=wcodes[:, g, lo:hi].bitcast(FP8X4),
+                rhs_scale=wscales[:, g, lo:hi],
+                start=(g == 0),
+                stop=(g == G - 1),
+            )
+
+        def s2(i):
+            accs[("s2", i)] = new_acc()
+            for k in range(2):
+                for g in range(G):
+                    s2_pass(i, g, k)
+
+        def finish(i):
+            b, t = divmod(i, NT)
+            acc = accs[("s2", i)]
+            osb = work.tile([P, O], F32, name="osb", bufs=3)
+            for k, (lo, hi) in enumerate(HALVES):
+                nc.vector.tensor_tensor(out=osb[:, lo:hi], in0=acc[k][:], in1=bias_bc[:, lo:hi], op=ALU.add)
+            nc.sync.dma_start(out=out[b].rearrange("(p t) o -> p t o", t=NT)[:, t, :], in_=osb[:])
+
+        x2_regroup(0, "vs")
+        x2_quantise(0)
+        w_regroup(0, "s")
+        s1(0)
+        s1(1)
+        x3(0)
+        x3(1)
+        s1(2)
+        s1(3)
+        x3(2)
+        x3(3)
+        transposes(0)
+        transposes(1)
+        w_regroup(3, "s")
+        transposes(2)
+        x2_regroup(1, "ss")
+        transposes(3)
+        w_quantise(0)
+        w_regroup(1, "v")
+        qx(0)
+        w_quantise(1)
+        w_regroup(2, "v")
+        w_quantise(2)
+        qx(1)
+        w_regroup(4, "v")
+        w_quantise(3)
+        w_quantise(4)
+        w_regroup(5, "v")
+        w_quantise(5)
+        accs[("s2", 0)] = new_acc()
+        accs[("s2", 1)] = new_acc()
+        for g in range(G):
+            for i in range(2):
+                for k in range(2):
+                    s2_pass(i, g, k)
+        x2_quantise(1)
+        qx(2)
+        finish(0)
+        s1(4)
+        finish(1)
+        s2(2)
+        x3(4)
+        qx(3)
+
+        for s in range(4, TILES + LAG + 1):
+            if 2 <= s - LAG - 1 < TILES:
+                finish(s - LAG - 1)
+            if 4 <= s - 1 < TILES:
+                qx(s - 1)
+            if s < TILES:
+                transposes(s)
+            if s + 1 < TILES:
+                s1(s + 1)
+                x3(s + 1)
+            if 3 <= s - LAG < TILES:
+                s2(s - LAG)
+            if s % NT == 1 and s // NT + 1 < B:
+                x2_regroup(s // NT + 1, "vv")
+                x2_quantise(s // NT + 1)

@@ -88,8 +88,18 @@ def tile_dgcn_pb_kernel(tc, x0, x1, x2, support, weights, biases, out):
             i_ap = src[:, :, lo:hi].rearrange("p t (c i) -> p c t i", i=4)
             if engine == "v":
                 nc.vector.tensor_copy(out=o_ap, in_=i_ap)
-            else:
+            elif engine == "s":
                 nc.scalar.copy(out=o_ap, in_=i_ap)
+            else:
+                for c0 in range(lo, hi, 256):
+                    nc.gpsimd.tensor_scalar(
+                        out=dst[:, c0:c0 + 256, :],
+                        in0=src[:, :, c0:c0 + 256].rearrange("p t c -> p c t"),
+                        scalar1=1.0,
+                        scalar2=0.0,
+                        op0=ALU.mult,
+                        op1=ALU.add,
+                    )
 
         def quantise(codes, scales, src):
             for lo, hi in HALVES:
@@ -276,5 +286,6 @@ def tile_dgcn_pb_kernel(tc, x0, x1, x2, support, weights, biases, out):
             if 3 <= s - LAG < TILES:
                 s2(s - LAG)
             if s % NT == 1 and s // NT + 1 < B:
-                x2_regroup(s // NT + 1, "vv")
+                x2_regroup(s // NT + 1, "gg")
+            if s % NT == 2 and s // NT + 1 < B:
                 x2_quantise(s // NT + 1)

@@ -178,7 +178,7 @@ def tile_dgcn_pb_kernel(tc, x0, x1, x2, support, weights, biases, out):
 
         grouped = {}
 
-        def transposes(i):
+        def transposes(i, engines="sss"):
             b, t = divmod(i, NT)
             gr = work.tile([P, G, P, 4], BF16, name="grouped", bufs=4, align_bytes=64)
             grouped[i] = gr
@@ -189,10 +189,16 @@ def tile_dgcn_pb_kernel(tc, x0, x1, x2, support, weights, biases, out):
                     for m in range(4):
                         src = xs[(m, b)] if m < 3 else x3s[b]
                         nc.tensor.transpose(bank[:, u, m, :], src[:, t, g * P:(g + 1) * P], ident_bf[:])
-                nc.scalar.copy(
-                    out=gr[:, 2 * gp:2 * gp + 2, :, :],
-                    in_=bank[:].rearrange("p u m r -> p u r m"),
-                )
+                if engines[gp] == "s":
+                    nc.scalar.copy(
+                        out=gr[:, 2 * gp:2 * gp + 2, :, :],
+                        in_=bank[:].rearrange("p u m r -> p u r m"),
+                    )
+                else:
+                    nc.vector.tensor_copy(
+                        out=gr[:, 2 * gp:2 * gp + 2, :, :],
+                        in_=bank[:].rearrange("p u m r -> p u r m"),
+                    )
 
         xq = {}
 
@@ -269,23 +275,33 @@ def tile_dgcn_pb_kernel(tc, x0, x1, x2, support, weights, biases, out):
         finish(0)
         s1(4)
         finish(1)
-        s2(2)
         x3(4)
+        s2(2)
         qx(3)
+        s1(5)
+        finish(2)
+        x3(5)
 
-        for s in range(4, TILES + LAG + 1):
-            if 2 <= s - LAG - 1 < TILES:
-                finish(s - LAG - 1)
-            if 4 <= s - 1 < TILES:
-                qx(s - 1)
-            if s < TILES:
-                transposes(s)
-            if s + 1 < TILES:
-                s1(s + 1)
-                x3(s + 1)
-            if 3 <= s - LAG < TILES:
-                s2(s - LAG)
-            if s % NT == 1 and s // NT + 1 < B:
-                x2_regroup(s // NT + 1, "gg")
-            if s % NT == 2 and s // NT + 1 < B:
-                x2_quantise(s // NT + 1)
+        for a in range(4, TILES + 2, 2):
+            nxt = a // NT + 1
+            if a % NT == 2 and nxt < B:
+                x2_quantise(nxt)
+            if a < TILES:
+                transposes(a, "svs")
+                transposes(a + 1)
+            if a + 2 < TILES:
+                s1(a + 2)
+                x3(a + 2)
+            if a < TILES:
+                qx(a)
+            s2(a - 1)
+            finish(a - 1)
+            if a < TILES:
+                qx(a + 1)
+                s2(a)
+                finish(a)
+            if a + 3 < TILES:
+                s1(a + 3)
+                x3(a + 3)
+            if a % NT == 0 and nxt < B:
+                x2_regroup(nxt, "gg")

@@ -230,10 +230,11 @@ def tile_dgcn_pb_kernel(tc, x0, x1, x2, support, weights, biases, out):
         def finish(i):
             b, t = divmod(i, NT)
             acc = accs[("s2", i)]
-            osb = work.tile([P, O], F32, name="osb", bufs=3)
+            rows = out[b].rearrange("(p t) o -> p t o", t=NT)
             for k, (lo, hi) in enumerate(HALVES):
-                nc.vector.tensor_tensor(out=osb[:, lo:hi], in0=acc[k][:], in1=bias_bc[:, lo:hi], op=ALU.add)
-            nc.sync.dma_start(out=out[b].rearrange("(p t) o -> p t o", t=NT)[:, t, :], in_=osb[:])
+                osb = work.tile([P, hi - lo], F32, name="osb%d" % k, bufs=3)
+                nc.vector.tensor_tensor(out=osb[:], in0=acc[k][:], in1=bias_bc[:, lo:hi], op=ALU.add)
+                nc.sync.dma_start(out=rows[:, t, lo:hi], in_=osb[:])
 
         x2_regroup(0, "vs")
         x2_quantise(0)
@@ -261,8 +262,8 @@ def tile_dgcn_pb_kernel(tc, x0, x1, x2, support, weights, biases, out):
         qx(1)
         w_regroup(4, "v")
         w_quantise(3)
-        w_quantise(4)
         w_regroup(5, "v")
+        w_quantise(4)
         w_quantise(5)
         accs[("s2", 0)] = new_acc()
         accs[("s2", 1)] = new_acc()

@@ -13,9 +13,8 @@ ALU = mybir.AluOpType
 P = 128
 B, N, D, O, M = 4, 512, 768, 768, 4
 NT = N // P
-G = D // P
 TILES = B * NT
-LAG = 2
+G = 3
 HALVES = ((0, 512), (512, 768))
 FLOPS = 2 * B * N * N * D + 2 * B * N * D * M * O
 
@@ -24,82 +23,91 @@ def tile_dgcn_pb_kernel(tc, x0, x1, x2, support, weights, biases, out):
     nc = tc.nc
     with ExitStack() as ctx:
         const = ctx.enter_context(tc.tile_pool(name="const", bufs=1))
-        big = ctx.enter_context(tc.tile_pool(name="big", bufs=12))
+        big = ctx.enter_context(tc.tile_pool(name="big", bufs=4))
         work = ctx.enter_context(tc.tile_pool(name="work", bufs=2))
         psum = ctx.enter_context(tc.psum_pool(name="psum", bufs=2))
         ctx.enter_context(tc.manual_schedule())
 
-        sup = const.tile([P, NT, N], BF16, name="sup")
-        nc.sync.dma_start(out=sup[:], in_=support.rearrange("(p t) j -> p t j", t=NT))
-        xs = {}
-        srcs = (x0, x1, x2)
+        xraw = {}
         wraw = {}
 
-        def load_x(m, b):
-            xt = big.tile([P, NT, D], BF16, name="x%d_%d" % (m, b), tag="big")
-            nc.sync.dma_start(out=xt[:], in_=srcs[m][b].rearrange("(p t) d -> p t d", t=NT))
-            xs[(m, b)] = xt
+        def load_x2(b):
+            xt = big.tile([P, NT, D], BF16, name="x2raw", bufs=3)
+            nc.sync.dma_start(out=xt[:], in_=x2[b].rearrange("(p t) d -> p t d", t=NT))
+            xraw[(2, b)] = xt
+
+        def load_x01(b):
+            xt = big.tile([P, 2, NT, D], BF16, name="x01_%d" % b, tag="big")
+            nc.sync.dma_start(out=xt[:, 1], in_=x1[b].rearrange("(p t) d -> p t d", t=NT))
+            nc.sync.dma_start(out=xt[:, 0], in_=x0[b].rearrange("(p t) d -> p t d", t=NT))
+            xraw[(1, b)] = xt[:, 1]
+            xraw[(0, b)] = xt[:, 0]
+
+        wview = weights.rearrange("(h q i r) o -> q h i (r o)", h=24, q=4, i=4)
 
         def load_w(g):
-            wr = big.tile([P, M, O], BF16, name="wraw%d" % g, tag="big")
-            nc.sync.dma_start(
-                out=wr[:],
-                in_=weights[g * P * M:(g + 1) * P * M, :].rearrange("(p t) o -> p t o", t=M),
-            )
+            wr = big.tile([P, 8 * O], BF16, name="wraw%d" % g, tag="big")
+            if g < 2:
+                for k in range(2):
+                    nc.sync.dma_start(out=wr[64 * k:64 * k + 64, :], in_=wview[2 * g + k, 0:16])
+            else:
+                for q in range(4):
+                    nc.sync.dma_start(out=wr[32 * q:32 * q + 32, :], in_=wview[q, 16:24])
             wraw[g] = wr
 
-        load_x(2, 0)
-        load_w(0)
-        load_x(1, 0)
-        load_x(0, 0)
-        for g in range(1, G):
+        load_x2(0)
+        sup = big.tile([P, NT, N], BF16, name="sup", tag="x2raw", bufs=3)
+        nc.sync.dma_start(out=sup[:], in_=support.rearrange("(p t) j -> p t j", t=NT))
+        load_x01(0)
+        for g in range(G):
             load_w(g)
-        for m in (2, 1, 0):
-            load_x(m, 1)
+        load_x2(1)
+        load_x01(1)
+        load_x2(2)
         bias_bc = const.tile([P, O], BF16, name="bias_bc")
         nc.sync.dma_start(out=bias_bc[:], in_=biases.partition_broadcast(P))
-        for b in range(2, B):
-            for m in (2, 1, 0):
-                load_x(m, b)
 
         ident_f = const.tile([P, P], F32, name="ident_f")
         make_identity(nc, ident_f[:])
-        ident_bf = const.tile([P, P], BF16, name="ident_bf")
-        make_identity(nc, ident_bf[:])
 
         supg = const.tile([P, NT * P * 4], BF16, name="supg", align_bytes=64)
         sup_codes = const.tile([P, N], U32, name="sup_codes", align_bytes=64)
         sup_scales = const.tile([P, N], U8, name="sup_scales", align_bytes=64)
-        sup_words = sup[:].bitcast(F32).rearrange("p t (q u) -> p t u q", u=2)
-        supg_words = supg[:].bitcast(F32).rearrange("q (t p u) -> q t p u", t=NT, u=2)
-        for half in range(2):
-            st = psum.tile([P, 2, 2, P], F32, name="st", tag="g", bufs=4)
-            for tt in range(2):
-                for u in range(2):
-                    nc.tensor.transpose(st[:, tt, u, :], sup_words[:, 2 * half + tt, u, :], ident_f[:])
-            nc.scalar.copy(
-                out=supg_words[:, 2 * half:2 * half + 2, :, :],
-                in_=st[:].rearrange("q t u p -> q t p u"),
-            )
-        nc.vector.quantize_mx(out=sup_codes[:].bitcast(FP8X4), scales=sup_scales[:], in_=supg[:])
 
-        def regroup(engine, dst, src, lo, hi):
-            o_ap = dst[:, lo:hi, :].rearrange("p (c i) t -> p c t i", i=4)
-            i_ap = src[:, :, lo:hi].rearrange("p t (c i) -> p c t i", i=4)
+        def sup_transposes():
+            sup_words = sup[:].bitcast(F32).rearrange("p t (q u) -> p t u q", u=2)
+            supg_words = supg[:].bitcast(F32).rearrange("q (t p u) -> q t p u", t=NT, u=2)
+            for half in range(2):
+                st = psum.tile([P, 2, 2, P], F32, name="st", tag="g", bufs=4)
+                for tt in range(2):
+                    for u in range(2):
+                        nc.tensor.transpose(st[:, tt, u, :], sup_words[:, 2 * half + tt, u, :], ident_f[:])
+                nc.scalar.copy(
+                    out=supg_words[:, 2 * half:2 * half + 2, :, :],
+                    in_=st[:].rearrange("q t u p -> q t p u"),
+                )
+
+        def sup_quantise():
+            nc.vector.quantize_mx(out=sup_codes[:].bitcast(FP8X4), scales=sup_scales[:], in_=supg[:])
+
+        def copy(engine, out_ap, in_ap):
             if engine == "v":
-                nc.vector.tensor_copy(out=o_ap, in_=i_ap)
-            elif engine == "s":
-                nc.scalar.copy(out=o_ap, in_=i_ap)
+                nc.vector.tensor_copy(out=out_ap, in_=in_ap)
             else:
-                for c0 in range(lo, hi, 256):
-                    nc.gpsimd.tensor_scalar(
-                        out=dst[:, c0:c0 + 256, :],
-                        in0=src[:, :, c0:c0 + 256].rearrange("p t c -> p c t"),
-                        scalar1=1.0,
-                        scalar2=0.0,
-                        op0=ALU.mult,
-                        op1=ALU.add,
-                    )
+                nc.scalar.copy(out=out_ap, in_=in_ap)
+
+        xp = {}
+
+        def perm(m, b, engines):
+            dst = work.tile([P, NT, D], BF16, name="x%dp" % m, align_bytes=64)
+            src = xraw[(m, b)]
+            for engine, (lo, hi) in zip(engines, HALVES):
+                copy(
+                    engine,
+                    dst[:, :, lo:hi].rearrange("p t (q h e) -> p t q h e", q=4, e=8),
+                    src[:, :, lo:hi].rearrange("p t (h q e) -> p t q h e", q=4, e=8),
+                )
+            xp[(m, b)] = dst
 
         def quantise(codes, scales, src):
             for lo, hi in HALVES:
@@ -113,9 +121,13 @@ def tile_dgcn_pb_kernel(tc, x0, x1, x2, support, weights, biases, out):
         x2q = {}
 
         def x2_regroup(b, engines):
-            x2g = work.tile([P, D, 4], BF16, name="x2g", align_bytes=64)
+            x2g = work.tile([P, D, 4], BF16, name="x2g", bufs=1, align_bytes=64)
             for engine, (lo, hi) in zip(engines, HALVES):
-                regroup(engine, x2g, xs[(2, b)], lo, hi)
+                copy(
+                    engine,
+                    x2g[:, lo:hi, :].rearrange("p (c i) t -> p c t i", i=4),
+                    xp[(2, b)][:, :, lo:hi].rearrange("p t (c i) -> p c t i", i=4),
+                )
             x2gs[b] = x2g
 
         def x2_quantise(b):
@@ -124,31 +136,42 @@ def tile_dgcn_pb_kernel(tc, x0, x1, x2, support, weights, biases, out):
             quantise(c, s, x2gs[b])
             x2q[b] = (c, s)
 
-        wcodes = const.tile([P, G, O], U32, name="wcodes", align_bytes=64)
-        wscales = const.tile([P, G, O], U8, name="wscales", align_bytes=64)
+        wcodes = const.tile([P, 2 * G, O], U32, name="wcodes", align_bytes=64)
+        wscales = const.tile([P, 2 * G, O], U8, name="wscales", align_bytes=64)
         wgs = {}
 
-        def w_regroup(g, engine):
-            wg = work.tile([P, O, 4], BF16, name="wg", bufs=4, align_bytes=64)
-            for lo, hi in HALVES:
-                regroup(engine, wg, wraw[g], lo, hi)
-            wgs[g] = wg
+        def w_regroup(j, k, engine):
+            g, a = divmod(j, 2)
+            lo, hi = HALVES[k]
+            wg = work.tile([P, hi - lo, 4], BF16, name="wg%d" % k, bufs=3 - k, align_bytes=64)
+            src = wraw[g][:].rearrange("p (e m o) -> p e m o", e=2, m=4)[:, :, 2 * a:2 * a + 2, lo:hi]
+            copy(
+                engine,
+                wg[:].rearrange("p (c i) (u e) -> p c u e i", i=4, u=2),
+                src.rearrange("p e u (c i) -> p c u e i", i=4),
+            )
+            wgs[(j, k)] = wg
 
-        def w_quantise(g):
-            quantise(wcodes[:, g, :], wscales[:, g, :], wgs[g])
+        def w_quantise(j, k):
+            lo, hi = HALVES[k]
+            nc.vector.quantize_mx(
+                out=wcodes[:, j, lo:hi].bitcast(FP8X4),
+                scales=wscales[:, j, lo:hi],
+                in_=wgs[(j, k)][:].rearrange("p c t -> p (c t)"),
+            )
 
-        x3s = {}
         accs = {}
 
-        def new_acc():
-            acc_a = psum.tile([P, 512], F32, name="acc_a")
-            acc_b = psum.tile([P, 256], F32, name="acc_b")
-            return acc_a, acc_b
+        def new_acc(k, tag=None):
+            lo, hi = HALVES[k]
+            if tag is None:
+                return psum.tile([P, hi - lo], F32, name="acc%d" % k)
+            return psum.tile([P, hi - lo], F32, name="acc%d" % k, tag=tag, bufs=4)
 
         def s1(i):
             b, t = divmod(i, NT)
             c, s = x2q[b]
-            acc = new_acc()
+            acc = [new_acc(0), new_acc(1)]
             for k, (lo, hi) in enumerate(HALVES):
                 nc.tensor.matmul_mx(
                     out=acc[k][:],
@@ -164,14 +187,14 @@ def tile_dgcn_pb_kernel(tc, x0, x1, x2, support, weights, biases, out):
         def x3(i):
             b, t = divmod(i, NT)
             if t == 0:
-                x3s[b] = work.tile([P, NT, D], BF16, name="x3t")
+                xp[(3, b)] = work.tile([P, NT, D], BF16, name="x3p", align_bytes=64)
             acc = accs[("s1", i)]
             for k, (lo, hi) in enumerate(HALVES):
                 nc.vector.scalar_tensor_tensor(
-                    out=x3s[b][:, t, lo:hi],
+                    out=xp[(3, b)][:, t, lo:hi],
                     in0=acc[k][:],
                     scalar=2.0,
-                    in1=xs[(1, b)][:, t, lo:hi],
+                    in1=xp[(1, b)][:, t, lo:hi],
                     op0=ALU.mult,
                     op1=ALU.subtract,
                 )
@@ -180,129 +203,173 @@ def tile_dgcn_pb_kernel(tc, x0, x1, x2, support, weights, biases, out):
 
         def transposes(i, engines="sss"):
             b, t = divmod(i, NT)
-            gr = work.tile([P, G, P, 4], BF16, name="grouped", bufs=4, align_bytes=64)
+            gr = work.tile([P, 2 * G, P, 4], BF16, name="grouped", bufs=3, align_bytes=64)
             grouped[i] = gr
-            for gp in range(G // 2):
-                bank = psum.tile([P, 2, 4, P], BF16, name="bank", tag="g", bufs=4)
-                for u in range(2):
-                    g = 2 * gp + u
-                    for m in range(4):
-                        src = xs[(m, b)] if m < 3 else x3s[b]
-                        nc.tensor.transpose(bank[:, u, m, :], src[:, t, g * P:(g + 1) * P], ident_bf[:])
-                if engines[gp] == "s":
-                    nc.scalar.copy(
-                        out=gr[:, 2 * gp:2 * gp + 2, :, :],
-                        in_=bank[:].rearrange("p u m r -> p u r m"),
-                    )
-                else:
-                    nc.vector.tensor_copy(
-                        out=gr[:, 2 * gp:2 * gp + 2, :, :],
-                        in_=bank[:].rearrange("p u m r -> p u r m"),
-                    )
+            words = gr[:].rearrange("p g r m -> p (g r m)").bitcast(F32).rearrange("p (g r u) -> p g r u", g=2 * G, u=2)
+            for g in range(G):
+                bank = psum.tile([P, 2, 2, P], F32, name="bank", tag="g", bufs=4)
+                for m in range(4):
+                    src = xp[(m, b)][:, t, 256 * g:256 * g + 256].bitcast(F32)
+                    nc.tensor.transpose(bank[:, m // 2, m % 2, :], src, ident_f[:])
+                copy(engines[g], words[:, 2 * g:2 * g + 2, :, :], bank[:].rearrange("p a u r -> p a r u"))
 
         xq = {}
 
         def qx(i):
-            c = work.tile([P, G * P], U32, name="xcodes", bufs=4, align_bytes=64)
-            s = work.tile([P, G * P], U8, name="xscales", bufs=4, align_bytes=64)
+            c = work.tile([P, 2 * G * P], U32, name="xcodes", bufs=6, align_bytes=64)
+            s = work.tile([P, 2 * G * P], U8, name="xscales", bufs=6, align_bytes=64)
             quantise(c, s, grouped[i][:].rearrange("p g r m -> p (g r) m"))
             xq[i] = (c, s)
 
-        def s2_pass(i, g, k):
+        def s2_pass(i, j, k):
             c, s = xq[i]
             lo, hi = HALVES[k]
             nc.tensor.matmul_mx(
-                out=accs[("s2", i)][k][:],
-                lhsT=c[:, g * P:(g + 1) * P].bitcast(FP8X4),
-                lhsT_scale=s[:, g * P:(g + 1) * P],
-                rhs=wcodes[:, g, lo:hi].bitcast(FP8X4),
-                rhs_scale=wscales[:, g, lo:hi],
-                start=(g == 0),
-                stop=(g == G - 1),
+                out=accs[(i, k)][:],
+                lhsT=c[:, j * P:(j + 1) * P].bitcast(FP8X4),
+                lhsT_scale=s[:, j * P:(j + 1) * P],
+                rhs=wcodes[:, j, lo:hi].bitcast(FP8X4),
+                rhs_scale=wscales[:, j, lo:hi],
+                start=(j == 0),
+                stop=(j == 2 * G - 1),
             )
 
+        def s2_half(i, k):
+            accs[(i, k)] = new_acc(k)
+            for j in range(2 * G):
+                s2_pass(i, j, k)
+
         def s2(i):
-            accs[("s2", i)] = new_acc()
-            for k in range(2):
-                for g in range(G):
-                    s2_pass(i, g, k)
+            s2_half(i, 0)
+            s2_half(i, 1)
+
+        def finish_half(i, k):
+            b, t = divmod(i, NT)
+            lo, hi = HALVES[k]
+            rows = out[b].rearrange("(p t) o -> p t o", t=NT)
+            osb = work.tile([P, hi - lo], F32, name="osb%d" % k, bufs=3)
+            nc.vector.tensor_tensor(out=osb[:], in0=accs[(i, k)][:], in1=bias_bc[:, lo:hi], op=ALU.add)
+            nc.sync.dma_start(out=rows[:, t, lo:hi], in_=osb[:])
 
         def finish(i):
-            b, t = divmod(i, NT)
-            acc = accs[("s2", i)]
-            rows = out[b].rearrange("(p t) o -> p t o", t=NT)
-            for k, (lo, hi) in enumerate(HALVES):
-                osb = work.tile([P, hi - lo], F32, name="osb%d" % k, bufs=3)
-                nc.vector.tensor_tensor(out=osb[:], in0=acc[k][:], in1=bias_bc[:, lo:hi], op=ALU.add)
-                nc.sync.dma_start(out=rows[:, t, lo:hi], in_=osb[:])
+            finish_half(i, 0)
+            finish_half(i, 1)
 
+        perm(2, 0, "vv")
         x2_regroup(0, "vs")
+        sup_transposes()
         x2_quantise(0)
-        w_regroup(0, "s")
-        s1(0)
-        s1(1)
-        x3(0)
-        x3(1)
-        s1(2)
-        s1(3)
-        x3(2)
-        x3(3)
-        transposes(0)
-        transposes(1)
-        w_regroup(3, "s")
-        transposes(2)
-        x2_regroup(1, "ss")
-        transposes(3)
-        w_quantise(0)
-        w_regroup(1, "v")
-        qx(0)
-        w_quantise(1)
-        w_regroup(2, "v")
-        w_quantise(2)
-        qx(1)
-        w_regroup(4, "v")
-        w_quantise(3)
-        w_regroup(5, "v")
-        w_quantise(4)
-        w_quantise(5)
-        accs[("s2", 0)] = new_acc()
-        accs[("s2", 1)] = new_acc()
-        for g in range(G):
-            for i in range(2):
-                for k in range(2):
-                    s2_pass(i, g, k)
-        x2_quantise(1)
-        qx(2)
-        finish(0)
-        s1(4)
-        finish(1)
-        x3(4)
-        s2(2)
-        qx(3)
-        s1(5)
-        finish(2)
-        x3(5)
+        perm(1, 0, "vv")
+        sup_quantise()
+        perm(0, 0, "ss")
+        for i in range(4):
+            s1(i)
+            x3(i)
+        for i in range(4):
+            transposes(i)
+        for i in range(4):
+            accs[(i, 0)] = new_acc(0, tag="g")
 
-        for a in range(4, TILES + 2, 2):
+        def some(j, tiles):
+            for i in tiles:
+                s2_pass(i, j, 0)
+
+        w_regroup(0, 0, "v")
+        w_regroup(1, 0, "v")
+        w_quantise(0, 0)
+        qx(0)
+        w_quantise(1, 0)
+        qx(1)
+        w_regroup(2, 0, "v")
+        qx(2)
+        w_quantise(2, 0)
+        w_regroup(3, 0, "v")
+        qx(3)
+        w_regroup(4, 0, "s")
+        w_regroup(5, 0, "s")
+        w_quantise(3, 0)
+        perm(2, 1, "vv")
+        w_quantise(4, 0)
+        x2_regroup(1, "vs")
+        w_quantise(5, 0)
+        for j in range(2):
+            some(j, (0, 1))
+        some(2, (0, 1))
+        for j in range(3):
+            some(j, (2, 3))
+        for j in range(3, 6):
+            some(j, (0, 1, 2, 3))
+        x2_quantise(1)
+        perm(1, 1, "ss")
+        perm(0, 1, "ss")
+        for i in range(2):
+            finish_half(i, 0)
+        s1(4)
+        s1(5)
+        x3(4)
+        x3(5)
+        for i in range(2, 4):
+            finish_half(i, 0)
+
+        transposes(4)
+        transposes(5)
+        s1(6)
+        w_regroup(0, 1, "v")
+        w_regroup(1, 1, "v")
+        qx(4)
+        w_quantise(0, 1)
+        w_quantise(1, 1)
+        for j in (2, 3, 4, 5):
+            w_regroup(j, 1, "s")
+        load_x01(2)
+        x3(6)
+        s2_half(4, 0)
+        s1(7)
+        qx(5)
+        w_quantise(2, 1)
+        w_quantise(3, 1)
+        x3(7)
+        w_quantise(4, 1)
+        w_quantise(5, 1)
+        for i in range(4):
+            s2_half(i, 1)
+        perm(2, 2, "vv")
+        x2_regroup(2, "ss")
+        for i in range(4):
+            finish_half(i, 1)
+        s2_half(4, 1)
+
+        for a in range(6, TILES + 2, 2):
             nxt = a // NT + 1
-            if a % NT == 2 and nxt < B:
+            first = a % NT == 0 and nxt < B
+            second = a % NT == 2 and nxt < B
+            if second:
                 x2_quantise(nxt)
+            finish(a - 2)
             if a < TILES:
-                transposes(a, "svs")
+                transposes(a)
                 transposes(a + 1)
+            if second:
+                perm(0, nxt, "ss")
+                perm(1, nxt, "vv")
+                if nxt + 1 < B:
+                    load_x2(nxt + 1)
+                    load_x01(nxt + 1)
             if a + 2 < TILES:
                 s1(a + 2)
-                x3(a + 2)
             if a < TILES:
                 qx(a)
+            if a + 2 < TILES:
+                x3(a + 2)
             s2(a - 1)
-            finish(a - 1)
             if a < TILES:
                 qx(a + 1)
-                s2(a)
-                finish(a)
+            if first:
+                perm(2, nxt, "vv")
+                x2_regroup(nxt, "ss")
+            finish(a - 1)
             if a + 3 < TILES:
                 s1(a + 3)
                 x3(a + 3)
-            if a % NT == 0 and nxt < B:
-                x2_regroup(nxt, "gg")
+            if a < TILES:
+                s2(a)

@@ -45,22 +45,23 @@ def tile_dgcn_pb_kernel(tc, x0, x1, x2, support, weights, biases, out):
 
         wview = weights.rearrange("(h q i r) o -> q h i (r o)", h=24, q=4, i=4)
 
-        def load_w(g):
-            wr = big.tile([P, 8 * O], BF16, name="wraw%d" % g, tag="big")
+        def load_w(g, upper):
+            queue = nc.scalar if upper else nc.sync
+            if not upper:
+                wraw[g] = big.tile([P, 8 * O], BF16, name="wraw%d" % g, tag="big")
+            wr = wraw[g]
             if g < 2:
-                for k in range(2):
-                    nc.sync.dma_start(out=wr[64 * k:64 * k + 64, :], in_=wview[2 * g + k, 0:16])
+                queue.dma_start(out=wr[64 * upper:64 * upper + 64, :], in_=wview[2 * g + upper, 0:16])
             else:
-                for q in range(4):
-                    nc.sync.dma_start(out=wr[32 * q:32 * q + 32, :], in_=wview[q, 16:24])
-            wraw[g] = wr
+                for q in range(2 * upper, 2 * upper + 2):
+                    queue.dma_start(out=wr[32 * q:32 * q + 32, :], in_=wview[q, 16:24])
 
         load_x2(0)
         sup = big.tile([P, NT, N], BF16, name="sup", tag="x2raw", bufs=3)
         nc.sync.dma_start(out=sup[:], in_=support.rearrange("(p t) j -> p t j", t=NT))
         load_x01(0)
         for g in range(G):
-            load_w(g)
+            load_w(g, 0)
         load_x2(1)
         load_x01(1)
         load_x2(2)
@@ -257,6 +258,8 @@ def tile_dgcn_pb_kernel(tc, x0, x1, x2, support, weights, biases, out):
 
         perm(2, 0, "vv")
         x2_regroup(0, "vs")
+        for g in range(G):
+            load_w(g, 1)
         sup_transposes()
         x2_quantise(0)
         perm(1, 0, "vv")

@@ -14,7 +14,7 @@ P = 128
 B, N, D, O, M = 4, 512, 768, 768, 4
 NT = N // P
 TILES = B * NT
-G = 3
+G = 6
 HALVES = ((0, 512), (512, 768))
 FLOPS = 2 * B * N * N * D + 2 * B * N * D * M * O
 
@@ -23,48 +23,40 @@ def tile_dgcn_pb_kernel(tc, x0, x1, x2, support, weights, biases, out):
     nc = tc.nc
     with ExitStack() as ctx:
         const = ctx.enter_context(tc.tile_pool(name="const", bufs=1))
-        big = ctx.enter_context(tc.tile_pool(name="big", bufs=4))
+        big = ctx.enter_context(tc.tile_pool(name="big", bufs=2))
         work = ctx.enter_context(tc.tile_pool(name="work", bufs=2))
         psum = ctx.enter_context(tc.psum_pool(name="psum", bufs=2))
         ctx.enter_context(tc.manual_schedule())
 
-        xraw = {}
+        x02 = {}
+        x13 = {}
         wraw = {}
 
         def load_x2(b):
-            xt = big.tile([P, NT, D], BF16, name="x2raw", bufs=3)
-            nc.sync.dma_start(out=xt[:], in_=x2[b].rearrange("(p t) d -> p t d", t=NT))
-            xraw[(2, b)] = xt
+            x02[b] = big.tile([P, 2, NT, D], BF16, name="x02")
+            nc.sync.dma_start(out=x02[b][:, 1], in_=x2[b].rearrange("(p t) d -> p t d", t=NT))
 
         def load_x01(b):
-            xt = big.tile([P, 2, NT, D], BF16, name="x01_%d" % b, tag="big")
-            nc.sync.dma_start(out=xt[:, 1], in_=x1[b].rearrange("(p t) d -> p t d", t=NT))
-            nc.sync.dma_start(out=xt[:, 0], in_=x0[b].rearrange("(p t) d -> p t d", t=NT))
-            xraw[(1, b)] = xt[:, 1]
-            xraw[(0, b)] = xt[:, 0]
+            x13[b] = big.tile([P, 2, NT, D], BF16, name="x13")
+            nc.sync.dma_start(out=x13[b][:, 0], in_=x1[b].rearrange("(p t) d -> p t d", t=NT))
+            nc.sync.dma_start(out=x02[b][:, 0], in_=x0[b].rearrange("(p t) d -> p t d", t=NT))
 
-        wview = weights.rearrange("(h q i r) o -> q h i (r o)", h=24, q=4, i=4)
+        wview = weights.rearrange("(g w e a u) o -> g e w a (u o)", g=G, w=64, e=2, a=2)
 
-        def load_w(g, upper):
-            queue = nc.scalar if upper else nc.sync
-            if not upper:
-                wraw[g] = big.tile([P, 8 * O], BF16, name="wraw%d" % g, tag="big")
-            wr = wraw[g]
-            if g < 2:
-                queue.dma_start(out=wr[64 * upper:64 * upper + 64, :], in_=wview[2 * g + upper, 0:16])
-            else:
-                for q in range(2 * upper, 2 * upper + 2):
-                    queue.dma_start(out=wr[32 * q:32 * q + 32, :], in_=wview[q, 16:24])
+        def load_w(g):
+            wr = big.tile([P, 2, 2 * O], BF16, name="wraw", bufs=6)
+            for e in range(2):
+                nc.sync.dma_start(out=wr[:, e, :], in_=wview[g, e])
+            wraw[g] = wr
 
-        load_x2(0)
-        sup = big.tile([P, NT, N], BF16, name="sup", tag="x2raw", bufs=3)
+        sup = const.tile([P, NT, N], BF16, name="sup")
         nc.sync.dma_start(out=sup[:], in_=support.rearrange("(p t) j -> p t j", t=NT))
+        load_x2(0)
         load_x01(0)
         for g in range(G):
-            load_w(g, 0)
+            load_w(g)
         load_x2(1)
         load_x01(1)
-        load_x2(2)
         bias_bc = const.tile([P, O], BF16, name="bias_bc")
         nc.sync.dma_start(out=bias_bc[:], in_=biases.partition_broadcast(P))
 
@@ -97,18 +89,18 @@ def tile_dgcn_pb_kernel(tc, x0, x1, x2, support, weights, biases, out):
             else:
                 nc.scalar.copy(out=out_ap, in_=in_ap)
 
-        xp = {}
+        pairs = {}
 
-        def perm(m, b, engines):
-            dst = work.tile([P, NT, D], BF16, name="x%dp" % m, align_bytes=64)
-            src = xraw[(m, b)]
-            for engine, (lo, hi) in zip(engines, HALVES):
-                copy(
-                    engine,
-                    dst[:, :, lo:hi].rearrange("p t (q h e) -> p t q h e", q=4, e=8),
-                    src[:, :, lo:hi].rearrange("p t (h q e) -> p t q h e", q=4, e=8),
-                )
-            xp[(m, b)] = dst
+        def pair(i, u, engine):
+            b, t = divmod(i, NT)
+            dst = work.tile([P, 2 * D], BF16, name="pair%d" % u, bufs=4, align_bytes=64)
+            src = (x13 if u else x02)[b][:, :, t, :]
+            copy(
+                engine,
+                dst[:].bitcast(F32).rearrange("p (w a) -> p w a", a=2),
+                src.bitcast(F32).rearrange("p a w -> p w a"),
+            )
+            pairs[(i, u)] = dst
 
         def quantise(codes, scales, src):
             for lo, hi in HALVES:
@@ -127,7 +119,7 @@ def tile_dgcn_pb_kernel(tc, x0, x1, x2, support, weights, biases, out):
                 copy(
                     engine,
                     x2g[:, lo:hi, :].rearrange("p (c i) t -> p c t i", i=4),
-                    xp[(2, b)][:, :, lo:hi].rearrange("p t (c i) -> p c t i", i=4),
+                    x02[b][:, 1, :, lo:hi].rearrange("p t (c i) -> p c t i", i=4),
                 )
             x2gs[b] = x2g
 
@@ -137,21 +129,20 @@ def tile_dgcn_pb_kernel(tc, x0, x1, x2, support, weights, biases, out):
             quantise(c, s, x2gs[b])
             x2q[b] = (c, s)
 
-        wcodes = const.tile([P, 2 * G, O], U32, name="wcodes", align_bytes=64)
-        wscales = const.tile([P, 2 * G, O], U8, name="wscales", align_bytes=64)
+        wcodes = const.tile([P, G, O], U32, name="wcodes", align_bytes=64)
+        wscales = const.tile([P, G, O], U8, name="wscales", align_bytes=64)
         wgs = {}
 
-        def w_regroup(j, k, engine):
-            g, a = divmod(j, 2)
+        def w_regroup(g, k, engine):
             lo, hi = HALVES[k]
             wg = work.tile([P, hi - lo, 4], BF16, name="wg%d" % k, bufs=3 - k, align_bytes=64)
-            src = wraw[g][:].rearrange("p (e m o) -> p e m o", e=2, m=4)[:, :, 2 * a:2 * a + 2, lo:hi]
+            src = wraw[g][:].rearrange("p e (u o) -> p e u o", u=2)[:, :, :, lo:hi]
             copy(
                 engine,
                 wg[:].rearrange("p (c i) (u e) -> p c u e i", i=4, u=2),
                 src.rearrange("p e u (c i) -> p c u e i", i=4),
             )
-            wgs[(j, k)] = wg
+            wgs[(g, k)] = wg
 
         def w_quantise(j, k):
             lo, hi = HALVES[k]
@@ -187,15 +178,13 @@ def tile_dgcn_pb_kernel(tc, x0, x1, x2, support, weights, biases, out):
 
         def x3(i):
             b, t = divmod(i, NT)
-            if t == 0:
-                xp[(3, b)] = work.tile([P, NT, D], BF16, name="x3p", align_bytes=64)
             acc = accs[("s1", i)]
             for k, (lo, hi) in enumerate(HALVES):
                 nc.vector.scalar_tensor_tensor(
-                    out=xp[(3, b)][:, t, lo:hi],
+                    out=x13[b][:, 1, t, lo:hi],
                     in0=acc[k][:],
                     scalar=2.0,
-                    in1=xp[(1, b)][:, t, lo:hi],
+                    in1=x13[b][:, 0, t, lo:hi],
                     op0=ALU.mult,
                     op1=ALU.subtract,
                 )
@@ -203,22 +192,23 @@ def tile_dgcn_pb_kernel(tc, x0, x1, x2, support, weights, biases, out):
         grouped = {}
 
         def transposes(i, engines="sss"):
-            b, t = divmod(i, NT)
-            gr = work.tile([P, 2 * G, P, 4], BF16, name="grouped", bufs=3, align_bytes=64)
+            gr = work.tile([P, G, P, 4], BF16, name="grouped", bufs=3, align_bytes=64)
             grouped[i] = gr
-            words = gr[:].rearrange("p g r m -> p (g r m)").bitcast(F32).rearrange("p (g r u) -> p g r u", g=2 * G, u=2)
-            for g in range(G):
+            words = gr[:].rearrange("p g r m -> p (g r m)").bitcast(F32).rearrange("p (g r u) -> p g r u", g=G, u=2)
+            for h in range(G // 2):
                 bank = psum.tile([P, 2, 2, P], F32, name="bank", tag="g", bufs=4)
-                for m in range(4):
-                    src = xp[(m, b)][:, t, 256 * g:256 * g + 256].bitcast(F32)
-                    nc.tensor.transpose(bank[:, m // 2, m % 2, :], src, ident_f[:])
-                copy(engines[g], words[:, 2 * g:2 * g + 2, :, :], bank[:].rearrange("p a u r -> p a r u"))
+                for k in range(2):
+                    for u in range(2):
+                        g = 2 * h + k
+                        src = pairs[(i, u)][:].bitcast(F32)[:, g * P:(g + 1) * P]
+                        nc.tensor.transpose(bank[:, k, u, :], src, ident_f[:])
+                copy(engines[h], words[:, 2 * h:2 * h + 2, :, :], bank[:].rearrange("p k u r -> p k r u"))
 
         xq = {}
 
         def qx(i):
-            c = work.tile([P, 2 * G * P], U32, name="xcodes", bufs=6, align_bytes=64)
-            s = work.tile([P, 2 * G * P], U8, name="xscales", bufs=6, align_bytes=64)
+            c = work.tile([P, G * P], U32, name="xcodes", bufs=6, align_bytes=64)
+            s = work.tile([P, G * P], U8, name="xscales", bufs=6, align_bytes=64)
             quantise(c, s, grouped[i][:].rearrange("p g r m -> p (g r) m"))
             xq[i] = (c, s)
 
@@ -232,12 +222,12 @@ def tile_dgcn_pb_kernel(tc, x0, x1, x2, support, weights, biases, out):
                 rhs=wcodes[:, j, lo:hi].bitcast(FP8X4),
                 rhs_scale=wscales[:, j, lo:hi],
                 start=(j == 0),
-                stop=(j == 2 * G - 1),
+                stop=(j == G - 1),
             )
 
         def s2_half(i, k):
             accs[(i, k)] = new_acc(k)
-            for j in range(2 * G):
+            for j in range(G):
                 s2_pass(i, j, k)
 
         def s2(i):
@@ -256,18 +246,21 @@ def tile_dgcn_pb_kernel(tc, x0, x1, x2, support, weights, biases, out):
             finish_half(i, 0)
             finish_half(i, 1)
 
-        perm(2, 0, "vv")
-        x2_regroup(0, "vs")
-        for g in range(G):
-            load_w(g, 1)
         sup_transposes()
-        x2_quantise(0)
-        perm(1, 0, "vv")
+        x2_regroup(0, "vs")
         sup_quantise()
-        perm(0, 0, "ss")
+        x2_quantise(0)
+        pair(0, 0, "s")
+        pair(1, 0, "s")
         for i in range(4):
             s1(i)
             x3(i)
+            if i % 2:
+                pair(i - 1, 1, "v")
+                pair(i, 1, "v")
+        pair(2, 0, "s")
+        w_regroup(0, 0, "s")
+        pair(3, 0, "s")
         for i in range(4):
             transposes(i)
         for i in range(4):
@@ -277,23 +270,21 @@ def tile_dgcn_pb_kernel(tc, x0, x1, x2, support, weights, biases, out):
             for i in tiles:
                 s2_pass(i, j, 0)
 
-        w_regroup(0, 0, "v")
         w_regroup(1, 0, "v")
         w_quantise(0, 0)
         qx(0)
         w_quantise(1, 0)
-        qx(1)
         w_regroup(2, 0, "v")
-        qx(2)
+        qx(1)
         w_quantise(2, 0)
         w_regroup(3, 0, "v")
-        qx(3)
+        qx(2)
         w_regroup(4, 0, "s")
         w_regroup(5, 0, "s")
         w_quantise(3, 0)
-        perm(2, 1, "vv")
-        w_quantise(4, 0)
+        qx(3)
         x2_regroup(1, "vs")
+        w_quantise(4, 0)
         w_quantise(5, 0)
         for j in range(2):
             some(j, (0, 1))
@@ -303,40 +294,48 @@ def tile_dgcn_pb_kernel(tc, x0, x1, x2, support, weights, biases, out):
         for j in range(3, 6):
             some(j, (0, 1, 2, 3))
         x2_quantise(1)
-        perm(1, 1, "ss")
-        perm(0, 1, "ss")
+        pair(4, 0, "s")
+        pair(5, 0, "s")
+        w_regroup(0, 1, "s")
+        w_regroup(1, 1, "s")
         for i in range(2):
             finish_half(i, 0)
         s1(4)
         s1(5)
         x3(4)
         x3(5)
+        pair(4, 1, "v")
+        pair(5, 1, "v")
         for i in range(2, 4):
             finish_half(i, 0)
 
         transposes(4)
         transposes(5)
         s1(6)
-        w_regroup(0, 1, "v")
-        w_regroup(1, 1, "v")
-        qx(4)
         w_quantise(0, 1)
         w_quantise(1, 1)
-        for j in (2, 3, 4, 5):
-            w_regroup(j, 1, "s")
+        w_regroup(2, 1, "v")
+        w_regroup(3, 1, "v")
+        qx(4)
+        w_quantise(2, 1)
+        w_quantise(3, 1)
+        w_regroup(4, 1, "s")
+        w_regroup(5, 1, "s")
+        pair(6, 0, "s")
+        pair(7, 0, "s")
+        load_x2(2)
         load_x01(2)
         x3(6)
         s2_half(4, 0)
         s1(7)
         qx(5)
-        w_quantise(2, 1)
-        w_quantise(3, 1)
-        x3(7)
+        pair(6, 1, "v")
         w_quantise(4, 1)
+        x3(7)
         w_quantise(5, 1)
+        pair(7, 1, "v")
         for i in range(4):
             s2_half(i, 1)
-        perm(2, 2, "vv")
         x2_regroup(2, "ss")
         for i in range(4):
             finish_half(i, 1)
@@ -352,12 +351,12 @@ def tile_dgcn_pb_kernel(tc, x0, x1, x2, support, weights, biases, out):
             if a < TILES:
                 transposes(a)
                 transposes(a + 1)
-            if second:
-                perm(0, nxt, "ss")
-                perm(1, nxt, "vv")
-                if nxt + 1 < B:
-                    load_x2(nxt + 1)
-                    load_x01(nxt + 1)
+            if a + 2 < TILES:
+                pair(a + 2, 0, "s")
+                pair(a + 3, 0, "s")
+            if second and nxt + 1 < B:
+                load_x2(nxt + 1)
+                load_x01(nxt + 1)
             if a + 2 < TILES:
                 s1(a + 2)
             if a < TILES:
@@ -365,14 +364,17 @@ def tile_dgcn_pb_kernel(tc, x0, x1, x2, support, weights, biases, out):
             if a + 2 < TILES:
                 x3(a + 2)
             s2(a - 1)
+            if first:
+                x2_regroup(nxt, "ss")
+            finish_half(a - 1, 0)
             if a < TILES:
                 qx(a + 1)
-            if first:
-                perm(2, nxt, "vv")
-                x2_regroup(nxt, "ss")
-            finish(a - 1)
+            finish_half(a - 1, 1)
             if a + 3 < TILES:
+                pair(a + 2, 1, "v")
                 s1(a + 3)
                 x3(a + 3)
             if a < TILES:
                 s2(a)
+            if a + 3 < TILES:
+                pair(a + 3, 1, "v")

@@ -34,12 +34,12 @@ def tile_dgcn_pb_kernel(tc, x0, x1, x2, support, weights, biases, out):
 
         def load_x2(b):
             x02[b] = big.tile([P, 2, NT, D], BF16, name="x02")
-            nc.sync.dma_start(out=x02[b][:, 1], in_=x2[b].rearrange("(p t) d -> p t d", t=NT))
+            nc.sync.dma_start(out=x02[b][:, 1].rearrange("p (u e) d -> p u e d", u=2), in_=x2[b].rearrange("(u p e) d -> p u e d", u=2, e=2))
 
         def load_x01(b):
+            nc.sync.dma_start(out=x02[b][:, 0].rearrange("p (u e) d -> p u e d", u=2), in_=x0[b].rearrange("(u p e) d -> p u e d", u=2, e=2))
             x13[b] = big.tile([P, 2, NT, D], BF16, name="x13")
-            nc.sync.dma_start(out=x13[b][:, 0], in_=x1[b].rearrange("(p t) d -> p t d", t=NT))
-            nc.sync.dma_start(out=x02[b][:, 0], in_=x0[b].rearrange("(p t) d -> p t d", t=NT))
+            nc.sync.dma_start(out=x13[b][:, 0].rearrange("p (u e) d -> p u e d", u=2), in_=x1[b].rearrange("(u p e) d -> p u e d", u=2, e=2))
 
         wview = weights.rearrange("(g w e a u) o -> g e w a (u o)", g=G, w=64, e=2, a=2)
 
@@ -49,9 +49,12 @@ def tile_dgcn_pb_kernel(tc, x0, x1, x2, support, weights, biases, out):
                 nc.sync.dma_start(out=wr[:, e, :], in_=wview[g, e])
             wraw[g] = wr
 
-        sup = const.tile([P, NT, N], BF16, name="sup")
-        nc.sync.dma_start(out=sup[:], in_=support.rearrange("(p t) j -> p t j", t=NT))
         load_x2(0)
+        sup = work.tile([P, NT, N], BF16, name="sup", tag="wg0", bufs=3, align_bytes=64)
+        nc.sync.dma_start(
+            out=sup[:].rearrange("p (u e) j -> p u e j", u=2),
+            in_=support.rearrange("(u p e) j -> p u e j", u=2, e=2),
+        )
         load_x01(0)
         for g in range(G):
             load_w(g)
@@ -63,12 +66,12 @@ def tile_dgcn_pb_kernel(tc, x0, x1, x2, support, weights, biases, out):
         ident_f = const.tile([P, P], F32, name="ident_f")
         make_identity(nc, ident_f[:])
 
-        supg = const.tile([P, NT * P * 4], BF16, name="supg", align_bytes=64)
+        supg = work.tile([P, NT * P * 4], BF16, name="supg", tag="wg0", bufs=3, align_bytes=64)
         sup_codes = const.tile([P, N], U32, name="sup_codes", align_bytes=64)
         sup_scales = const.tile([P, N], U8, name="sup_scales", align_bytes=64)
 
         def sup_transposes():
-            sup_words = sup[:].bitcast(F32).rearrange("p t (q u) -> p t u q", u=2)
+            sup_words = sup[:].bitcast(F32).rearrange("p t (u q) -> p t u q", u=2)
             supg_words = supg[:].bitcast(F32).rearrange("q (t p u) -> q t p u", t=NT, u=2)
             for half in range(2):
                 st = psum.tile([P, 2, 2, P], F32, name="st", tag="g", bufs=4)
@@ -93,7 +96,7 @@ def tile_dgcn_pb_kernel(tc, x0, x1, x2, support, weights, biases, out):
 
         def pair(i, u, engine):
             b, t = divmod(i, NT)
-            dst = work.tile([P, 2 * D], BF16, name="pair%d" % u, bufs=4, align_bytes=64)
+            dst = work.tile([P, 2 * D], BF16, name="pair%d" % u, bufs=4 - u, align_bytes=64)
             src = (x13 if u else x02)[b][:, :, t, :]
             copy(
                 engine,
@@ -135,7 +138,7 @@ def tile_dgcn_pb_kernel(tc, x0, x1, x2, support, weights, biases, out):
 
         def w_regroup(g, k, engine):
             lo, hi = HALVES[k]
-            wg = work.tile([P, hi - lo, 4], BF16, name="wg%d" % k, bufs=3 - k, align_bytes=64)
+            wg = work.tile([P, hi - lo, 4], BF16, name="wg%d" % k, bufs=3 + k, align_bytes=64)
             src = wraw[g][:].rearrange("p e (u o) -> p e u o", u=2)[:, :, :, lo:hi]
             copy(
                 engine,
@@ -156,9 +159,8 @@ def tile_dgcn_pb_kernel(tc, x0, x1, x2, support, weights, biases, out):
 
         def new_acc(k, tag=None):
             lo, hi = HALVES[k]
-            if tag is None:
-                return psum.tile([P, hi - lo], F32, name="acc%d" % k)
-            return psum.tile([P, hi - lo], F32, name="acc%d" % k, tag=tag, bufs=4)
+            tag = tag or "acc%d" % k
+            return psum.tile([P, hi - lo], F32, name="acc%d" % k, tag=tag, bufs=4 if tag == "g" else 2)
 
         def s1(i):
             b, t = divmod(i, NT)
@@ -207,8 +209,8 @@ def tile_dgcn_pb_kernel(tc, x0, x1, x2, support, weights, biases, out):
         xq = {}
 
         def qx(i):
-            c = work.tile([P, G * P], U32, name="xcodes", bufs=6, align_bytes=64)
-            s = work.tile([P, G * P], U8, name="xscales", bufs=6, align_bytes=64)
+            c = work.tile([P, G * P], U32, name="xcodes", bufs=8, align_bytes=64)
+            s = work.tile([P, G * P], U8, name="xscales", bufs=8, align_bytes=64)
             quantise(c, s, grouped[i][:].rearrange("p g r m -> p (g r) m"))
             xq[i] = (c, s)
 
@@ -237,34 +239,34 @@ def tile_dgcn_pb_kernel(tc, x0, x1, x2, support, weights, biases, out):
         def finish_half(i, k):
             b, t = divmod(i, NT)
             lo, hi = HALVES[k]
-            rows = out[b].rearrange("(p t) o -> p t o", t=NT)
-            osb = work.tile([P, hi - lo], F32, name="osb%d" % k, bufs=3)
+            rows = out[b].rearrange("(u p e) o -> p u e o", u=2, e=2)
+            osb = work.tile([P, hi - lo], F32, name="osb%d" % k, bufs=3 + k)
             nc.vector.tensor_tensor(out=osb[:], in0=accs[(i, k)][:], in1=bias_bc[:, lo:hi], op=ALU.add)
-            nc.sync.dma_start(out=rows[:, t, lo:hi], in_=osb[:])
+            nc.sync.dma_start(out=rows[:, t // 2, t % 2, lo:hi], in_=osb[:])
 
         def finish(i):
             finish_half(i, 0)
             finish_half(i, 1)
 
-        sup_transposes()
         x2_regroup(0, "vs")
-        sup_quantise()
+        sup_transposes()
         x2_quantise(0)
-        pair(0, 0, "s")
-        pair(1, 0, "s")
+        pair(0, 0, "v")
+        sup_quantise()
+        pair(1, 0, "v")
+        pair(2, 0, "s")
+        pair(3, 0, "s")
         for i in range(4):
             s1(i)
             x3(i)
             if i % 2:
                 pair(i - 1, 1, "v")
                 pair(i, 1, "v")
-        pair(2, 0, "s")
         w_regroup(0, 0, "s")
-        pair(3, 0, "s")
         for i in range(4):
             transposes(i)
         for i in range(4):
-            accs[(i, 0)] = new_acc(0, tag="g")
+            accs[(i, 0)] = new_acc(0, ("acc0", "acc1", "g", "g")[i])
 
         def some(j, tiles):
             for i in tiles:
@@ -277,7 +279,7 @@ def tile_dgcn_pb_kernel(tc, x0, x1, x2, support, weights, biases, out):
         w_regroup(2, 0, "v")
         qx(1)
         w_quantise(2, 0)
-        w_regroup(3, 0, "v")
+        w_regroup(3, 0, "s")
         qx(2)
         w_regroup(4, 0, "s")
         w_regroup(5, 0, "s")
@@ -298,83 +300,62 @@ def tile_dgcn_pb_kernel(tc, x0, x1, x2, support, weights, biases, out):
         pair(5, 0, "s")
         w_regroup(0, 1, "s")
         w_regroup(1, 1, "s")
-        for i in range(2):
-            finish_half(i, 0)
-        s1(4)
-        s1(5)
-        x3(4)
-        x3(5)
-        pair(4, 1, "v")
-        pair(5, 1, "v")
-        for i in range(2, 4):
-            finish_half(i, 0)
-
-        transposes(4)
-        transposes(5)
-        s1(6)
-        w_quantise(0, 1)
-        w_quantise(1, 1)
-        w_regroup(2, 1, "v")
-        w_regroup(3, 1, "v")
-        qx(4)
-        w_quantise(2, 1)
-        w_quantise(3, 1)
-        w_regroup(4, 1, "s")
-        w_regroup(5, 1, "s")
-        pair(6, 0, "s")
-        pair(7, 0, "s")
+        w_regroup(2, 1, "s")
         load_x2(2)
         load_x01(2)
-        x3(6)
-        s2_half(4, 0)
-        s1(7)
-        qx(5)
-        pair(6, 1, "v")
-        w_quantise(4, 1)
-        x3(7)
-        w_quantise(5, 1)
-        pair(7, 1, "v")
-        for i in range(4):
-            s2_half(i, 1)
-        x2_regroup(2, "ss")
-        for i in range(4):
-            finish_half(i, 1)
-        s2_half(4, 1)
+        s1(4)
+        finish_half(0, 0)
+        x3(4)
+        finish_half(1, 0)
+        pair(4, 1, "v")
+        s1(5)
+        finish_half(2, 0)
+        x3(5)
+        finish_half(3, 0)
+        transposes(4)
+        w_quantise(0, 1)
+        pair(5, 1, "v")
+        w_quantise(1, 1)
+        w_quantise(2, 1)
+        w_regroup(3, 1, "v")
+        qx(4)
 
-        for a in range(6, TILES + 2, 2):
-            nxt = a // NT + 1
-            first = a % NT == 0 and nxt < B
-            second = a % NT == 2 and nxt < B
-            if second:
-                x2_quantise(nxt)
-            finish(a - 2)
-            if a < TILES:
-                transposes(a)
-                transposes(a + 1)
-            if a + 2 < TILES:
-                pair(a + 2, 0, "s")
-                pair(a + 3, 0, "s")
-            if second and nxt + 1 < B:
-                load_x2(nxt + 1)
-                load_x01(nxt + 1)
-            if a + 2 < TILES:
-                s1(a + 2)
-            if a < TILES:
-                qx(a)
-            if a + 2 < TILES:
-                x3(a + 2)
-            s2(a - 1)
-            if first:
-                x2_regroup(nxt, "ss")
-            finish_half(a - 1, 0)
-            if a < TILES:
-                qx(a + 1)
-            finish_half(a - 1, 1)
-            if a + 3 < TILES:
-                pair(a + 2, 1, "v")
-                s1(a + 3)
-                x3(a + 3)
-            if a < TILES:
-                s2(a)
-            if a + 3 < TILES:
-                pair(a + 3, 1, "v")
+        late = {4: (0, 1), 5: (2, 3), 6: (4, 5, 6)}
+        for i in range(4, TILES):
+            nxt = i // NT + 1
+            if i > 4:
+                for n in late.get(i - 1, (i - 1,)):
+                    finish_half(n, 1)
+            if i + 1 < TILES:
+                transposes(i + 1)
+            if i + 2 < TILES:
+                s1(i + 2)
+            s2_half(i, 0)
+            if i + 2 < TILES:
+                pair(i + 2, 0, "s")
+            if i == 4:
+                w_regroup(4, 1, "v")
+                w_regroup(5, 1, "s")
+            if i + 2 < TILES:
+                x3(i + 2)
+            if i == 4:
+                w_quantise(3, 1)
+            if i + 1 < TILES:
+                qx(i + 1)
+            if i == 4:
+                w_quantise(4, 1)
+                w_quantise(5, 1)
+            if i + 2 < TILES:
+                pair(i + 2, 1, "v")
+            if nxt < B:
+                if i % NT == 2 and nxt + 1 < B:
+                    load_x2(nxt + 1)
+                    load_x01(nxt + 1)
+                if i % NT == 0:
+                    x2_regroup(nxt, "vs")
+                if i % NT == 1:
+                    x2_quantise(nxt)
+            finish_half(i, 0)
+            for n in late.get(i, (i,)):
+                s2_half(n, 1)
+        finish_half(TILES - 1, 1)

@@ -240,7 +240,7 @@ def tile_dgcn_pb_kernel(tc, x0, x1, x2, support, weights, biases, out):
             b, t = divmod(i, NT)
             lo, hi = HALVES[k]
             rows = out[b].rearrange("(u p e) o -> p u e o", u=2, e=2)
-            osb = work.tile([P, hi - lo], F32, name="osb%d" % k, bufs=3 + k)
+            osb = work.tile([P, hi - lo], F32, name="osb%d" % k, bufs=4)
             nc.vector.tensor_tensor(out=osb[:], in0=accs[(i, k)][:], in1=bias_bc[:, lo:hi], op=ALU.add)
             nc.sync.dma_start(out=rows[:, t // 2, t % 2, lo:hi], in_=osb[:])
 
@@ -276,56 +276,74 @@ def tile_dgcn_pb_kernel(tc, x0, x1, x2, support, weights, biases, out):
         w_quantise(0, 0)
         qx(0)
         w_quantise(1, 0)
-        w_regroup(2, 0, "v")
         qx(1)
+        w_regroup(2, 0, "v")
+        qx(2)
         w_quantise(2, 0)
         w_regroup(3, 0, "s")
-        qx(2)
         w_regroup(4, 0, "s")
         w_regroup(5, 0, "s")
-        w_quantise(3, 0)
         qx(3)
-        x2_regroup(1, "vs")
+        w_quantise(3, 0)
+        x2_regroup(1, "vv")
+        x2_quantise(1)
         w_quantise(4, 0)
         w_quantise(5, 0)
         for j in range(2):
             some(j, (0, 1))
-        some(2, (0, 1))
+        for j in range(2):
+            some(j, (2,))
+        some(2, (0, 1, 2))
         for j in range(3):
-            some(j, (2, 3))
-        for j in range(3, 6):
+            some(j, (3,))
+        some(3, (0, 1, 2, 3))
+        s1(4)
+        for j in range(4, 6):
             some(j, (0, 1, 2, 3))
-        x2_quantise(1)
         pair(4, 0, "s")
-        pair(5, 0, "s")
+        x3(4)
         w_regroup(0, 1, "s")
+        finish_half(0, 0)
+        pair(4, 1, "v")
+        finish_half(2, 0)
+        pair(5, 0, "s")
+        transposes(4)
+        finish_half(1, 0)
+        s1(5)
         w_regroup(1, 1, "s")
         w_regroup(2, 1, "s")
         load_x2(2)
         load_x01(2)
-        s1(4)
-        finish_half(0, 0)
-        x3(4)
-        finish_half(1, 0)
-        pair(4, 1, "v")
-        s1(5)
-        finish_half(2, 0)
-        x3(5)
         finish_half(3, 0)
-        transposes(4)
+        x3(5)
         w_quantise(0, 1)
         pair(5, 1, "v")
+        qx(4)
         w_quantise(1, 1)
         w_quantise(2, 1)
+        w_regroup(5, 1, "s")
         w_regroup(3, 1, "v")
-        qx(4)
+        w_regroup(4, 1, "v")
+        transposes(5)
+        s1(6)
+        s2_half(4, 0)
+        pair(6, 0, "s")
+        for j in range(3, 6):
+            w_quantise(j, 1)
+        x3(6)
+        qx(5)
+        pair(6, 1, "v")
+        finish_half(4, 0)
+        for i in (0, 1, 2, 3):
+            s2_half(i, 1)
 
-        late = {4: (0, 1), 5: (2, 3), 6: (4, 5, 6)}
-        for i in range(4, TILES):
+        late = {4: (0, 1, 2, 3), 5: (4, 5)}
+        for i in range(5, TILES):
             nxt = i // NT + 1
-            if i > 4:
-                for n in late.get(i - 1, (i - 1,)):
-                    finish_half(n, 1)
+            for n in late.get(i - 1, (i - 1,)):
+                finish_half(n, 1)
+            if i == 5:
+                x2_regroup(2, "vs")
             if i + 1 < TILES:
                 transposes(i + 1)
             if i + 2 < TILES:
@@ -333,18 +351,9 @@ def tile_dgcn_pb_kernel(tc, x0, x1, x2, support, weights, biases, out):
             s2_half(i, 0)
             if i + 2 < TILES:
                 pair(i + 2, 0, "s")
-            if i == 4:
-                w_regroup(4, 1, "v")
-                w_regroup(5, 1, "s")
-            if i + 2 < TILES:
                 x3(i + 2)
-            if i == 4:
-                w_quantise(3, 1)
             if i + 1 < TILES:
                 qx(i + 1)
-            if i == 4:
-                w_quantise(4, 1)
-                w_quantise(5, 1)
             if i + 2 < TILES:
                 pair(i + 2, 1, "v")
             if nxt < B:

@@ -121,8 +121,8 @@ def tile_dgcn_pb_kernel(tc, x0, x1, x2, support, weights, biases, out):
             for engine, (lo, hi) in zip(engines, HALVES):
                 copy(
                     engine,
-                    x2g[:, lo:hi, :].rearrange("p (c i) t -> p c t i", i=4),
-                    x02[b][:, 1, :, lo:hi].rearrange("p t (c i) -> p c t i", i=4),
+                    x2g[:, lo:hi, :].rearrange("p (c i) t -> p c t i", i=8),
+                    x02[b][:, 1, :, lo:hi].rearrange("p t (c i) -> p c t i", i=8),
                 )
             x2gs[b] = x2g
 
@@ -142,8 +142,8 @@ def tile_dgcn_pb_kernel(tc, x0, x1, x2, support, weights, biases, out):
             src = wraw[g][:].rearrange("p e (u o) -> p e u o", u=2)[:, :, :, lo:hi]
             copy(
                 engine,
-                wg[:].rearrange("p (c i) (u e) -> p c u e i", i=4, u=2),
-                src.rearrange("p e u (c i) -> p c u e i", i=4),
+                wg[:].rearrange("p (c i) (u e) -> p c u e i", i=8, u=2),
+                src.rearrange("p e u (c i) -> p c u e i", i=8),
             )
             wgs[(g, k)] = wg
 

@@ -70,11 +70,17 @@ def tile_dgcn_pb_kernel(tc, x0, x1, x2, support, weights, biases, out):
         sup_codes = const.tile([P, N], U32, name="sup_codes", align_bytes=64)
         sup_scales = const.tile([P, N], U8, name="sup_scales", align_bytes=64)
 
-        def sup_transposes():
+        def keep_warm(bank, n):
+            for k in range(n):
+                nc.tensor.matmul(out=bank, lhsT=ident_f[:], rhs=ident_f[:], start=True, stop=True)
+
+        def sup_transposes(warm):
             sup_words = sup[:].bitcast(F32).rearrange("p t (u q) -> p t u q", u=2)
             supg_words = supg[:].bitcast(F32).rearrange("q (t p u) -> q t p u", t=NT, u=2)
             for half in range(2):
                 st = psum.tile([P, 2, 2, P], F32, name="st", tag="g", bufs=4)
+                if half == 0:
+                    keep_warm(st[:, 0, 0, :], warm)
                 for tt in range(2):
                     for u in range(2):
                         nc.tensor.transpose(st[:, tt, u, :], sup_words[:, 2 * half + tt, u, :], ident_f[:])
@@ -162,10 +168,11 @@ def tile_dgcn_pb_kernel(tc, x0, x1, x2, support, weights, biases, out):
             tag = tag or "acc%d" % k
             return psum.tile([P, hi - lo], F32, name="acc%d" % k, tag=tag, bufs=4 if tag == "g" else 2)
 
-        def s1(i):
+        def s1(i, warm=0):
             b, t = divmod(i, NT)
             c, s = x2q[b]
             acc = [new_acc(0), new_acc(1)]
+            keep_warm(acc[0][:, 0:P], warm)
             for k, (lo, hi) in enumerate(HALVES):
                 nc.tensor.matmul_mx(
                     out=acc[k][:],
@@ -193,12 +200,13 @@ def tile_dgcn_pb_kernel(tc, x0, x1, x2, support, weights, biases, out):
 
         grouped = {}
 
-        def transposes(i, engines="sss"):
+        def transposes(i, engines="sss", warm=(0, 0, 0)):
             gr = work.tile([P, G, P, 4], BF16, name="grouped", bufs=3, align_bytes=64)
             grouped[i] = gr
             words = gr[:].rearrange("p g r m -> p (g r m)").bitcast(F32).rearrange("p (g r u) -> p g r u", g=G, u=2)
             for h in range(G // 2):
                 bank = psum.tile([P, 2, 2, P], F32, name="bank", tag="g", bufs=4)
+                keep_warm(bank[:, 0, 0, :], warm[h])
                 for k in range(2):
                     for u in range(2):
                         g = 2 * h + k
@@ -249,7 +257,7 @@ def tile_dgcn_pb_kernel(tc, x0, x1, x2, support, weights, biases, out):
             finish_half(i, 1)
 
         x2_regroup(0, "vs")
-        sup_transposes()
+        sup_transposes(6)
         x2_quantise(0)
         pair(0, 0, "v")
         sup_quantise()
@@ -257,14 +265,14 @@ def tile_dgcn_pb_kernel(tc, x0, x1, x2, support, weights, biases, out):
         pair(2, 0, "s")
         pair(3, 0, "s")
         for i in range(4):
-            s1(i)
+            s1(i, 3 if i == 0 else 0)
             x3(i)
             if i % 2:
                 pair(i - 1, 1, "v")
                 pair(i, 1, "v")
         w_regroup(0, 0, "s")
         for i in range(4):
-            transposes(i)
+            transposes(i, warm=(0, 1, 1))
         for i in range(4):
             accs[(i, 0)] = new_acc(0, ("acc0", "acc1", "g", "g")[i])
 
@@ -297,7 +305,7 @@ def tile_dgcn_pb_kernel(tc, x0, x1, x2, support, weights, biases, out):
         for j in range(3):
             some(j, (3,))
         some(3, (0, 1, 2, 3))
-        s1(4)
+        s1(4, 2)
         for j in range(4, 6):
             some(j, (0, 1, 2, 3))
         pair(4, 0, "s")
@@ -324,7 +332,7 @@ def tile_dgcn_pb_kernel(tc, x0, x1, x2, support, weights, biases, out):
         w_regroup(5, 1, "s")
         w_regroup(3, 1, "v")
         w_regroup(4, 1, "v")
-        transposes(5)
+        transposes(5, warm=(4, 0, 0))
         s1(6)
         s2_half(4, 0)
         pair(6, 0, "s")

@@ -312,7 +312,7 @@ def tile_dgcn_pb_kernel(tc, x0, x1, x2, support, weights, biases, out):
         x3(4)
         w_regroup(0, 1, "s")
         finish_half(0, 0)
-        pair(4, 1, "v")
+        pair(4, 1, "s")
         finish_half(2, 0)
         pair(5, 0, "s")
         transposes(4)
@@ -338,14 +338,18 @@ def tile_dgcn_pb_kernel(tc, x0, x1, x2, support, weights, biases, out):
         pair(6, 0, "s")
         for j in range(3, 6):
             w_quantise(j, 1)
+        s2_half(0, 1)
+        s2_half(1, 1)
         x3(6)
+        finish_half(0, 1)
+        finish_half(1, 1)
         qx(5)
-        pair(6, 1, "v")
+        pair(6, 1, "s")
         finish_half(4, 0)
-        for i in (0, 1, 2, 3):
-            s2_half(i, 1)
+        s2_half(2, 1)
+        s2_half(3, 1)
 
-        late = {4: (0, 1, 2, 3), 5: (4, 5)}
+        late = {4: (2, 3), 5: (4, 5)}
         for i in range(5, TILES):
             nxt = i // NT + 1
             for n in late.get(i - 1, (i - 1,)):

from contextlib import ExitStack

import concourse.mybir as mybir
from concourse.masks import make_identity

FP8X4 = mybir.dt.float8_e4m3fn_x4
BF16 = mybir.dt.bfloat16
F32 = mybir.dt.float32
U32 = mybir.dt.uint32
U8 = mybir.dt.uint8
ALU = mybir.AluOpType

P = 128
B, N, D, O, M = 4, 512, 768, 768, 4
NT = N // P
TILES = B * NT
G = 6
HALVES = ((0, 512), (512, 768))
FLOPS = 2 * B * N * N * D + 2 * B * N * D * M * O


def tile_dgcn_pb_kernel(tc, x0, x1, x2, support, weights, biases, out):
    nc = tc.nc
    with ExitStack() as ctx:
        const = ctx.enter_context(tc.tile_pool(name="const", bufs=1))
        big = ctx.enter_context(tc.tile_pool(name="big", bufs=2))
        work = ctx.enter_context(tc.tile_pool(name="work", bufs=2))
        psum = ctx.enter_context(tc.psum_pool(name="psum", bufs=2))
        ctx.enter_context(tc.manual_schedule())

        x02 = {}
        x13 = {}
        wraw = {}

        def load_x2(b):
            x02[b] = big.tile([P, 2, NT, D], BF16, name="x02")
            nc.sync.dma_start(out=x02[b][:, 1].rearrange("p (u e) d -> p u e d", u=2), in_=x2[b].rearrange("(u p e) d -> p u e d", u=2, e=2))

        def load_x01(b):
            nc.sync.dma_start(out=x02[b][:, 0].rearrange("p (u e) d -> p u e d", u=2), in_=x0[b].rearrange("(u p e) d -> p u e d", u=2, e=2))
            x13[b] = big.tile([P, 2, NT, D], BF16, name="x13")
            nc.sync.dma_start(out=x13[b][:, 0].rearrange("p (u e) d -> p u e d", u=2), in_=x1[b].rearrange("(u p e) d -> p u e d", u=2, e=2))

        wview = weights.rearrange("(g w e a u) o -> g e w a (u o)", g=G, w=64, e=2, a=2)

        def load_w(g):
            wr = big.tile([P, 2, 2 * O], BF16, name="wraw", bufs=6)
            for e in range(2):
                nc.sync.dma_start(out=wr[:, e, :], in_=wview[g, e])
            wraw[g] = wr

        load_x2(0)
        sup = work.tile([P, NT, N], BF16, name="sup", tag="wg0", bufs=3, align_bytes=64)
        nc.sync.dma_start(
            out=sup[:].rearrange("p (u e) j -> p u e j", u=2),
            in_=support.rearrange("(u p e) j -> p u e j", u=2, e=2),
        )
        load_x01(0)
        for g in range(G):
            load_w(g)
        load_x2(1)
        load_x01(1)
        bias_bc = const.tile([P, O], BF16, name="bias_bc")
        nc.sync.dma_start(out=bias_bc[:], in_=biases.partition_broadcast(P))

        ident_f = const.tile([P, P], F32, name="ident_f")
        make_identity(nc, ident_f[:])

        supg = work.tile([P, NT * P * 4], BF16, name="supg", tag="wg0", bufs=3, align_bytes=64)
        sup_codes = const.tile([P, N], U32, name="sup_codes", align_bytes=64)
        sup_scales = const.tile([P, N], U8, name="sup_scales", align_bytes=64)

        def keep_warm(bank, n):
            for k in range(n):
                nc.tensor.matmul(out=bank, lhsT=ident_f[:], rhs=ident_f[:], start=True, stop=True)

        def sup_transposes(warm):
            sup_words = sup[:].bitcast(F32).rearrange("p t (u q) -> p t u q", u=2)
            supg_words = supg[:].bitcast(F32).rearrange("q (t p u) -> q t p u", t=NT, u=2)
            for half in range(2):
                st = psum.tile([P, 2, 2, P], F32, name="st", tag="g", bufs=4)
                if half == 0:
                    keep_warm(st[:, 0, 0, :], warm)
                for tt in range(2):
                    for u in range(2):
                        nc.tensor.transpose(st[:, tt, u, :], sup_words[:, 2 * half + tt, u, :], ident_f[:])
                nc.scalar.copy(
                    out=supg_words[:, 2 * half:2 * half + 2, :, :],
                    in_=st[:].rearrange("q t u p -> q t p u"),
                )

        def sup_quantise():
            nc.vector.quantize_mx(out=sup_codes[:].bitcast(FP8X4), scales=sup_scales[:], in_=supg[:])

        def copy(engine, out_ap, in_ap):
            if engine == "v":
                nc.vector.tensor_copy(out=out_ap, in_=in_ap)
            else:
                nc.scalar.copy(out=out_ap, in_=in_ap)

        pairs = {}

        def pair(i, u, engine):
            b, t = divmod(i, NT)
            dst = work.tile([P, 2 * D], BF16, name="pair%d" % u, bufs=4 - u, align_bytes=64)
            src = (x13 if u else x02)[b][:, :, t, :]
            copy(
                engine,
                dst[:].bitcast(F32).rearrange("p (w a) -> p w a", a=2),
                src.bitcast(F32).rearrange("p a w -> p w a"),
            )
            pairs[(i, u)] = dst

        def quantise(codes, scales, src):
            for lo, hi in HALVES:
                nc.vector.quantize_mx(
                    out=codes[:, lo:hi].bitcast(FP8X4),
                    scales=scales[:, lo:hi],
                    in_=src[:, lo:hi, :].rearrange("p c t -> p (c t)"),
                )

        x2gs = {}
        x2q = {}

        def x2_regroup(b, engines):
            x2g = work.tile([P, D, 4], BF16, name="x2g", bufs=1, align_bytes=64)
            for engine, (lo, hi) in zip(engines, HALVES):
                copy(
                    engine,
                    x2g[:, lo:hi, :].rearrange("p (c i) t -> p c t i", i=8),
                    x02[b][:, 1, :, lo:hi].rearrange("p t (c i) -> p c t i", i=8),
                )
            x2gs[b] = x2g

        def x2_quantise(b):
            c = work.tile([P, D], U32, name="x2codes", align_bytes=64)
            s = work.tile([P, D], U8, name="x2scales", align_bytes=64)
            quantise(c, s, x2gs[b])
            x2q[b] = (c, s)

        wcodes = const.tile([P, G, O], U32, name="wcodes", align_bytes=64)
        wscales = const.tile([P, G, O], U8, name="wscales", align_bytes=64)
        wgs = {}

        def w_regroup(g, k, engine):
            lo, hi = HALVES[k]
            wg = work.tile([P, hi - lo, 4], BF16, name="wg%d" % k, bufs=3 + k, align_bytes=64)
            src = wraw[g][:].rearrange("p e (u o) -> p e u o", u=2)[:, :, :, lo:hi]
            copy(
                engine,
                wg[:].rearrange("p (c i) (u e) -> p c u e i", i=8, u=2),
                src.rearrange("p e u (c i) -> p c u e i", i=8),
            )
            wgs[(g, k)] = wg

        def w_quantise(j, k):
            lo, hi = HALVES[k]
            nc.vector.quantize_mx(
                out=wcodes[:, j, lo:hi].bitcast(FP8X4),
                scales=wscales[:, j, lo:hi],
                in_=wgs[(j, k)][:].rearrange("p c t -> p (c t)"),
            )

        accs = {}

        def new_acc(k, tag=None):
            lo, hi = HALVES[k]
            tag = tag or "acc%d" % k
            return psum.tile([P, hi - lo], F32, name="acc%d" % k, tag=tag, bufs=4 if tag == "g" else 2)

        def s1(i, warm=0):
            b, t = divmod(i, NT)
            c, s = x2q[b]
            acc = [new_acc(0), new_acc(1)]
            keep_warm(acc[0][:, 0:P], warm)
            for k, (lo, hi) in enumerate(HALVES):
                nc.tensor.matmul_mx(
                    out=acc[k][:],
                    lhsT=sup_codes[:, t * P:(t + 1) * P].bitcast(FP8X4),
                    lhsT_scale=sup_scales[:, t * P:(t + 1) * P],
                    rhs=c[:, lo:hi].bitcast(FP8X4),
                    rhs_scale=s[:, lo:hi],
                    start=True,
                    stop=True,
                )
            accs[("s1", i)] = acc

        def x3(i):
            b, t = divmod(i, NT)
            acc = accs[("s1", i)]
            for k, (lo, hi) in enumerate(HALVES):
                nc.vector.scalar_tensor_tensor(
                    out=x13[b][:, 1, t, lo:hi],
                    in0=acc[k][:],
                    scalar=2.0,
                    in1=x13[b][:, 0, t, lo:hi],
                    op0=ALU.mult,
                    op1=ALU.subtract,
                )

        grouped = {}

        def transposes(i, engines="sss", warm=(0, 0, 0)):
            gr = work.tile([P, G, P, 4], BF16, name="grouped", bufs=3, align_bytes=64)
            grouped[i] = gr
            words = gr[:].rearrange("p g r m -> p (g r m)").bitcast(F32).rearrange("p (g r u) -> p g r u", g=G, u=2)
            for h in range(G // 2):
                bank = psum.tile([P, 2, 2, P], F32, name="bank", tag="g", bufs=4)
                keep_warm(bank[:, 0, 0, :], warm[h])
                for k in range(2):
                    for u in range(2):
                        g = 2 * h + k
                        src = pairs[(i, u)][:].bitcast(F32)[:, g * P:(g + 1) * P]
                        nc.tensor.transpose(bank[:, k, u, :], src, ident_f[:])
                copy(engines[h], words[:, 2 * h:2 * h + 2, :, :], bank[:].rearrange("p k u r -> p k r u"))

        xq = {}

        def qx(i):
            c = work.tile([P, G * P], U32, name="xcodes", bufs=8, align_bytes=64)
            s = work.tile([P, G * P], U8, name="xscales", bufs=8, align_bytes=64)
            quantise(c, s, grouped[i][:].rearrange("p g r m -> p (g r) m"))
            xq[i] = (c, s)

        def s2_pass(i, j, k):
            c, s = xq[i]
            lo, hi = HALVES[k]
            nc.tensor.matmul_mx(
                out=accs[(i, k)][:],
                lhsT=c[:, j * P:(j + 1) * P].bitcast(FP8X4),
                lhsT_scale=s[:, j * P:(j + 1) * P],
                rhs=wcodes[:, j, lo:hi].bitcast(FP8X4),
                rhs_scale=wscales[:, j, lo:hi],
                start=(j == 0),
                stop=(j == G - 1),
            )

        def s2_half(i, k):
            accs[(i, k)] = new_acc(k)
            for j in range(G):
                s2_pass(i, j, k)

        def s2(i):
            s2_half(i, 0)
            s2_half(i, 1)

        def finish_half(i, k):
            b, t = divmod(i, NT)
            lo, hi = HALVES[k]
            rows = out[b].rearrange("(u p e) o -> p u e o", u=2, e=2)
            osb = work.tile([P, hi - lo], F32, name="osb%d" % k, bufs=4)
            nc.vector.tensor_tensor(out=osb[:], in0=accs[(i, k)][:], in1=bias_bc[:, lo:hi], op=ALU.add)
            nc.sync.dma_start(out=rows[:, t // 2, t % 2, lo:hi], in_=osb[:])

        def finish(i):
            finish_half(i, 0)
            finish_half(i, 1)

        x2_regroup(0, "vs")
        sup_transposes(6)
        x2_quantise(0)
        pair(0, 0, "v")
        sup_quantise()
        pair(1, 0, "v")
        pair(2, 0, "s")
        pair(3, 0, "s")
        for i in range(4):
            s1(i, 3 if i == 0 else 0)
            x3(i)
            if i % 2:
                pair(i - 1, 1, "v")
                pair(i, 1, "v")
        w_regroup(0, 0, "s")
        for i in range(4):
            transposes(i, warm=(0, 1, 1))
        for i in range(4):
            accs[(i, 0)] = new_acc(0, ("acc0", "acc1", "g", "g")[i])

        def some(j, tiles):
            for i in tiles:
                s2_pass(i, j, 0)

        w_regroup(1, 0, "v")
        w_quantise(0, 0)
        qx(0)
        w_quantise(1, 0)
        qx(1)
        w_regroup(2, 0, "v")
        qx(2)
        w_quantise(2, 0)
        w_regroup(3, 0, "s")
        w_regroup(4, 0, "s")
        w_regroup(5, 0, "s")
        qx(3)
        w_quantise(3, 0)
        x2_regroup(1, "vv")
        x2_quantise(1)
        w_quantise(4, 0)
        w_quantise(5, 0)
        for j in range(2):
            some(j, (0, 1))
        for j in range(2):
            some(j, (2,))
        some(2, (0, 1, 2))
        for j in range(3):
            some(j, (3,))
        some(3, (0, 1, 2, 3))
        s1(4, 2)
        for j in range(4, 6):
            some(j, (0, 1, 2, 3))
        pair(4, 0, "s")
        x3(4)
        w_regroup(0, 1, "s")
        finish_half(0, 0)
        pair(4, 1, "s")
        finish_half(2, 0)
        pair(5, 0, "s")
        transposes(4)
        finish_half(1, 0)
        s1(5)
        w_regroup(1, 1, "s")
        w_regroup(2, 1, "s")
        load_x2(2)
        load_x01(2)
        finish_half(3, 0)
        x3(5)
        w_quantise(0, 1)
        pair(5, 1, "v")
        qx(4)
        w_quantise(1, 1)
        w_quantise(2, 1)
        w_regroup(5, 1, "s")
        w_regroup(3, 1, "v")
        w_regroup(4, 1, "v")
        transposes(5, warm=(4, 0, 0))
        s1(6)
        s2_half(4, 0)
        pair(6, 0, "s")
        for j in range(3, 6):
            w_quantise(j, 1)
        s2_half(0, 1)
        s2_half(1, 1)
        x3(6)
        finish_half(0, 1)
        finish_half(1, 1)
        qx(5)
        pair(6, 1, "s")
        finish_half(4, 0)
        s2_half(2, 1)
        s2_half(3, 1)

        late = {4: (2, 3), 5: (4, 5)}
        for i in range(5, TILES):
            nxt = i // NT + 1
            for n in late.get(i - 1, (i - 1,)):
                finish_half(n, 1)
            if i == 5:
                x2_regroup(2, "vs")
            if i + 1 < TILES:
                transposes(i + 1)
            if i + 2 < TILES:
                s1(i + 2)
            s2_half(i, 0)
            if i + 2 < TILES:
                pair(i + 2, 0, "s")
                x3(i + 2)
            if i + 1 < TILES:
                qx(i + 1)
            if i + 2 < TILES:
                pair(i + 2, 1, "v")
            if nxt < B:
                if i % NT == 2 and nxt + 1 < B:
                    load_x2(nxt + 1)
                    load_x01(nxt + 1)
                if i % NT == 0:
                    x2_regroup(nxt, "vs")
                if i % NT == 1:
                    x2_quantise(nxt)
            finish_half(i, 0)
            for n in late.get(i, (i,)):
                s2_half(n, 1)
        finish_half(TILES - 1, 1)
